import numpy as np
import ml_dtypes


def mxq(x, axis, fmt="e4m3"):
    dtype, down = {"e4m3": (ml_dtypes.float8_e4m3fn, 7), "e5m2": (ml_dtypes.float8_e5m2, 14)}[fmt]
    v = np.moveaxis(np.asarray(x, np.float32).astype(ml_dtypes.bfloat16).astype(np.float64), axis, -1)
    blocks = v.reshape(v.shape[:-1] + (-1, 32))
    amax = np.abs(blocks).max(-1, keepdims=True)
    byte = np.maximum(np.where(amax > 0, np.frexp(amax)[1] - 1 + 127, 0) - down, 1)
    scale = np.exp2(byte - 127.0)
    codes = (blocks / scale).astype(np.float32).astype(dtype).astype(np.float64)
    return np.moveaxis((codes * scale).reshape(v.shape), -1, axis)


WIDE = False


def mx_kscale(k):
    if not WIDE:
        return np.ones(k)
    levels = np.array([10, -10, 5, -5, 0])
    a = np.random.permutation(np.resize(levels, k // 512 * 4)).reshape(k // 512, 4)
    idx = np.arange(k)
    return np.exp2(a[idx // 512, idx % 128 // 32])


BF16 = ml_dtypes.bfloat16


def bf(x):
    return np.asarray(x, np.float32).astype(BF16)


def f64(x):
    return np.asarray(x).astype(np.float64)


E2M1 = np.array([0.0, 0.5, 1.0, 1.5, 2.0, 3.0, 4.0, 6.0, -0.0, -0.5, -1.0, -1.5, -2.0, -3.0, -4.0, -6.0])


def pack_weight(w, fmt):
    k, n = w.shape
    w = f64(bf(w)).reshape(k // 32, 32, n)
    amax = np.abs(w).max(1)
    if fmt == "e4m3":
        byte = np.frexp(amax)[1] - 1 + 127 - 7
    else:
        mant, ex = np.frexp(amax / 6.0)
        byte = np.where(mant > 0.5, ex, ex - 1) + 127
    byte = np.clip(np.where(amax > 0, byte, 1), 1, 254)
    scaled = (w * np.exp2(127.0 - byte)[:, None, :]).reshape(k, n).astype(np.float32)
    by_word = np.ascontiguousarray(scaled.reshape(k // 512, 128, 4, n).transpose(0, 1, 3, 2))
    if fmt == "e4m3":
        words = by_word.astype(ml_dtypes.float8_e4m3fn).view(np.uint8)
    else:
        c = by_word.astype(ml_dtypes.float4_e2m1fn).view(np.uint8) & 0xF
        words = c[..., 0::2] | (c[..., 1::2] << 4)
    return np.ascontiguousarray(words), np.ascontiguousarray(byte.astype(np.uint8).reshape(k // 512, 16, n))


def unpack_weight(words, scales, fmt):
    g, p, n, _ = words.shape
    if fmt == "e4m3":
        vals = np.ascontiguousarray(words).view(ml_dtypes.float8_e4m3fn).astype(np.float64)
    else:
        nib = np.empty((g, p, n, 4), np.uint8)
        nib[..., 0::2] = words & 0xF
        nib[..., 1::2] = words >> 4
        vals = E2M1[nib]
    vals = vals * np.repeat(np.exp2(scales.astype(np.float64) - 127.0), 8, axis=1)[..., None]
    return vals.transpose(0, 1, 3, 2).reshape(g * 512, n)


B, L, S, D, H = 2, 384, 128, 1024, 8
HD = D // H
T = S + L
EPS = 1e-6
FMT = "e4m3"


def rmsnorm(t, w):
    return t / np.sqrt(np.mean(t * t, axis=-1, keepdims=True) + EPS) * w


def to_mha(t):
    return t.reshape(t.shape[0], t.shape[1], H, HD).transpose(0, 2, 1, 3)


def apply_rope(t, cos, sin):
    tr, ti = t[..., 0::2], t[..., 1::2]
    return np.stack([tr * cos - ti * sin, tr * sin + ti * cos], axis=-1).reshape(t.shape)


def pre_qk(t, Wqk_words, Wqk_scales, qn, kn):
    qk = mxq(f64(t), 2, "e4m3") @ unpack_weight(Wqk_words, Wqk_scales, FMT)
    q, k = qk[..., :D], qk[..., D:]
    return rmsnorm(to_mha(q), f64(qn)), rmsnorm(to_mha(k), f64(kn))


def setup_inputs():
    s = mx_kscale(D)
    inv = 1.0 / (10000.0 ** (np.arange(0, HD, 2) / HD))
    off = np.random.randint(0, T, (B, 1, 1))
    ang = (np.arange(T)[None, :, None] + off) * inv[None, None, :]
    x = bf(np.random.standard_normal((B, L, D)) * s)
    c = bf(np.random.standard_normal((B, S, D)) * s)
    freqs_cis = bf(np.stack([np.cos(ang), np.sin(ang)], axis=-1))
    Wqk_x_words, Wqk_x_scales = pack_weight(np.random.standard_normal((D, 2 * D)) / np.sqrt(D) / s[:, None], FMT)
    qn_x = bf(1.0 + 0.1 * np.random.standard_normal(HD))
    kn_x = bf(1.0 + 0.1 * np.random.standard_normal(HD))
    Wqk_c_words, Wqk_c_scales = pack_weight(np.random.standard_normal((D, 2 * D)) / np.sqrt(D) / s[:, None], FMT)
    qn_c = bf(1.0 + 0.1 * np.random.standard_normal(HD))
    kn_c = bf(1.0 + 0.1 * np.random.standard_normal(HD))
    return {
        "x": x,
        "c": c,
        "freqs_cis": freqs_cis,
        "Wqk_x_words": Wqk_x_words,
        "Wqk_x_scales": Wqk_x_scales,
        "qn_x": qn_x,
        "kn_x": kn_x,
        "Wqk_c_words": Wqk_c_words,
        "Wqk_c_scales": Wqk_c_scales,
        "qn_c": qn_c,
        "kn_c": kn_c,
    }


def reference(x, c, freqs_cis, Wqk_x_words, Wqk_x_scales, qn_x, kn_x, Wqk_c_words, Wqk_c_scales, qn_c, kn_c):
    qc, kc = pre_qk(c, Wqk_c_words, Wqk_c_scales, qn_c, kn_c)
    qx, kx = pre_qk(x, Wqk_x_words, Wqk_x_scales, qn_x, kn_x)
    q = np.concatenate([qc, qx], axis=2)
    k = np.concatenate([kc, kx], axis=2)
    f = f64(freqs_cis)
    cos = f[..., 0][:, None]
    sin = f[..., 1][:, None]
    return apply_rope(q, cos, sin), apply_rope(k, cos, sin)

@@ -1,0 +1,236 @@
+from contextlib import ExitStack
+
+import concourse.mybir as mybir
+from concourse.masks import make_identity
+
+F32 = mybir.dt.float32
+BF16 = mybir.dt.bfloat16
+I32 = mybir.dt.int32
+U32 = mybir.dt.uint32
+U8 = mybir.dt.uint8
+FP8X4 = mybir.dt.float8_e4m3fn_x4
+MULT = mybir.AluOpType.mult
+ADD = mybir.AluOpType.add
+SQUARE = mybir.ActivationFunctionType.Square
+SQRT = mybir.ActivationFunctionType.Sqrt
+
+P = 128
+BATCH = 2
+LEN_C = 128
+LEN_X = 384
+K = 1024
+K_PASS = 512
+PASSES = K // K_PASS
+N = 2048
+HEAD = 128
+PAIRS = HEAD // 2
+BANK = 512
+HEADS_PER_BANK = BANK // HEAD
+BANKS_PER_OUTPUT = N // 2 // BANK
+X_TILES = LEN_X // P
+TOKEN_TILES = BATCH * (X_TILES + 1)
+EPS = 1e-6
+
+FLOPS = 2 * BATCH * (LEN_C + LEN_X) * K * N
+
+
+def pairs(ap):
+    if ap.ndim == 2:
+        return ap.rearrange("p (j e) -> p j e", e=2)
+    return ap.rearrange("p t (j e) -> p t j e", e=2)
+
+
+def tile_dualstreamattentionwithrotaryembedding_pa_kernel(
+    tc,
+    x,
+    c,
+    freqs_cis,
+    Wqk_x_words,
+    Wqk_x_scales,
+    qn_x,
+    kn_x,
+    Wqk_c_words,
+    Wqk_c_scales,
+    qn_c,
+    kn_c,
+    out_0,
+    out_1,
+):
+    nc = tc.nc
+    outputs = (out_0, out_1)
+    given_words = {"x": Wqk_x_words, "c": Wqk_c_words}
+    given_scales = {"x": Wqk_x_scales, "c": Wqk_c_scales}
+    gain_vectors = (qn_x, kn_x, qn_c, kn_c)
+    first_gain = {"x": 0, "c": 2}
+
+    groups = [("x", b, X_TILES * b, X_TILES, LEN_C) for b in range(BATCH)]
+    groups += [("c", b, X_TILES * BATCH + b, 1, 0) for b in range(BATCH)]
+
+    with ExitStack() as ctx:
+        keep = ctx.enter_context(tc.tile_pool(name="keep", bufs=1))
+        work = ctx.enter_context(tc.tile_pool(name="work", bufs=3))
+        psum = ctx.enter_context(tc.psum_pool(name="psum", bufs=8))
+
+        tokens = keep.tile([P, TOKEN_TILES, K], BF16)
+        freqs = keep.tile([P, TOKEN_TILES, HEAD], BF16)
+        words = {s: keep.tile([P, PASSES, 4 * N], U8, name="words_" + s, align_bytes=64) for s in "xc"}
+        planes = {s: keep.tile([P, N], U8, name="planes_" + s, align_bytes=64) for s in "xc"}
+        gain_rows = keep.tile([P, len(gain_vectors) * HEAD], BF16)
+        ones = keep.tile([P, P], BF16)
+        identity = keep.tile([P, P], F32)
+
+        for s in "xc":
+            nc.vector.memset(planes[s][:].bitcast(I32), 0)
+        nc.vector.memset(gain_rows[:], 0.0)
+        nc.vector.memset(ones[:], 1.0)
+        make_identity(nc, identity[:])
+
+        def load_x(b):
+            nc.sync.dma_start(
+                out=tokens[:, X_TILES * b : X_TILES * (b + 1), :],
+                in_=x[b].rearrange("(p i) k -> p i k", i=X_TILES),
+            )
+
+        def load_scales(s):
+            for q in range(4):
+                nc.sync.dma_start(
+                    out=planes[s][32 * q : 32 * q + 4 * PASSES, :].bitcast(I32),
+                    in_=given_scales[s][:, 4 * q : 4 * q + 4, :].bitcast(I32),
+                )
+
+        def load_words(s, bank):
+            byte_cols = slice(4 * BANK * bank, 4 * BANK * (bank + 1))
+            nc.sync.dma_start(
+                out=words[s][:, :, byte_cols].bitcast(I32),
+                in_=given_words[s].rearrange("g p n t -> p g (n t)")[:, :, byte_cols].bitcast(I32),
+            )
+
+        load_x(0)
+        load_scales("x")
+        for bank in range(N // BANK):
+            load_words("x", bank)
+        load_x(1)
+        nc.sync.dma_start(out=tokens[:, X_TILES * BATCH :, :], in_=c.rearrange("b p k -> p b k"))
+        load_scales("c")
+        for bank in range(N // BANK):
+            load_words("c", bank)
+
+        for v, vector in enumerate(gain_vectors):
+            nc.scalar.dma_start(
+                out=gain_rows[0:1, HEAD * v : HEAD * (v + 1)],
+                in_=vector.rearrange("(o d) -> o d", o=1),
+            )
+        nc.scalar.dma_start(
+            out=freqs[:, : X_TILES * BATCH, :].rearrange("p (b i) d -> p b (i d)", b=BATCH),
+            in_=freqs_cis[:, LEN_C:, :, :].rearrange("b (p i) j e -> p b (i j e)", i=X_TILES),
+        )
+        nc.scalar.dma_start(
+            out=freqs[:, X_TILES * BATCH :, :],
+            in_=freqs_cis[:, :LEN_C, :, :].rearrange("b p j e -> p b (j e)"),
+        )
+
+        gain_bank = psum.tile([P, BANK], F32, tag="bank")
+        nc.tensor.matmul(out=gain_bank[:], lhsT=ones[:], rhs=gain_rows[:], start=True, stop=True)
+        gains = keep.tile([P, len(gain_vectors), HEAD], F32)
+        nc.scalar.copy(out=gains[:].rearrange("p v d -> p (v d)"), in_=gain_bank[:])
+
+        turned = keep.tile([P, TOKEN_TILES, HEAD], BF16)
+        nc.scalar.mul(out=pairs(turned[:])[:, :, :, 0:1], in_=pairs(freqs[:])[:, :, :, 1:2], mul=-1.0)
+        nc.scalar.copy(out=pairs(turned[:])[:, :, :, 1:2], in_=pairs(freqs[:])[:, :, :, 0:1])
+
+        table = keep.tile([P, TOKEN_TILES, 2, 2, HEAD], F32)
+        codes = keep.tile([P, TOKEN_TILES, PASSES * P], U32, align_bytes=64)
+        code_scales = keep.tile([P, TOKEN_TILES, PASSES * P], U8, align_bytes=64)
+
+        def prepare(group):
+            s, b, first_tile, tiles, first_position = group
+            for t in range(first_tile, first_tile + tiles):
+                token_words = tokens[:, t, :].bitcast(F32)
+                flipped = psum.tile([P, PASSES * 2, P], F32, tag="bank")
+                for g in range(PASSES):
+                    for u in range(2):
+                        nc.tensor.transpose(
+                            flipped[:, 2 * g + u, :],
+                            token_words[:, 256 * g + u : 256 * (g + 1) : 2],
+                            identity[:],
+                        )
+                grouped = work.tile([P, K], BF16, align_bytes=64)
+                nc.scalar.copy(
+                    out=grouped[:].bitcast(F32).rearrange("p (g r u) -> p g r u", g=PASSES, u=2),
+                    in_=flipped[:].rearrange("p (g u) r -> p g r u", u=2),
+                )
+                nc.vector.quantize_mx(
+                    out=codes[:, t, :].bitcast(FP8X4), scales=code_scales[:, t, :], in_=grouped[:]
+                )
+            these = slice(first_tile, first_tile + tiles)
+            for w in range(2):
+                gain = pairs(gains[:, first_gain[s] + w, :])
+                for e, angles in enumerate((freqs, turned)):
+                    nc.gpsimd.tensor_tensor(
+                        out=pairs(table[:, these, w, e, :]),
+                        in0=pairs(angles[:, these, :]),
+                        in1=gain[:, :, e : e + 1].unsqueeze(1).to_broadcast([P, tiles, PAIRS, 2]),
+                        op=MULT,
+                    )
+
+        def project_norm_rotate(s, t, bank, result):
+            w = bank // BANKS_PER_OUTPUT
+            acc = psum.tile([P, BANK], F32, tag="bank")
+            for g in range(PASSES):
+                nc.tensor.matmul_mx(
+                    out=acc[:],
+                    lhsT=codes[:, t, P * g : P * (g + 1)].bitcast(FP8X4),
+                    lhsT_scale=code_scales[:, t, P * g : P * (g + 1)],
+                    rhs=words[s][:, g, 4 * BANK * bank : 4 * BANK * (bank + 1)].bitcast(FP8X4),
+                    rhs_scale=planes[s][4 * g : P, BANK * bank : BANK * (bank + 1)],
+                    start=(g == 0),
+                    stop=(g == PASSES - 1),
+                )
+            squares = work.tile([P, BANK], F32)
+            sum_squares = work.tile([P, HEADS_PER_BANK], F32)
+            for h in range(HEADS_PER_BANK):
+                nc.scalar.activation(
+                    out=squares[:, HEAD * h : HEAD * (h + 1)],
+                    in_=acc[:, HEAD * h : HEAD * (h + 1)],
+                    func=SQUARE,
+                    accum_out=sum_squares[:, h : h + 1],
+                )
+            rms = work.tile([P, HEADS_PER_BANK], F32)
+            nc.scalar.activation(out=rms[:], in_=sum_squares[:], func=SQRT, scale=1.0 / HEAD, bias=EPS)
+            r = work.tile([P, HEADS_PER_BANK], F32)
+            nc.vector.reciprocal(out=r[:], in_=rms[:])
+            from_even = work.tile([P, HEADS_PER_BANK, HEAD], F32)
+            from_odd = work.tile([P, HEADS_PER_BANK, HEAD], F32)
+            for h in range(HEADS_PER_BANK):
+                head = pairs(acc[:, HEAD * h : HEAD * (h + 1)])
+                for e, product in enumerate((from_even, from_odd)):
+                    nc.vector.scalar_tensor_tensor(
+                        out=pairs(product[:, h, :]),
+                        in0=head[:, :, e : e + 1].to_broadcast([P, PAIRS, 2]),
+                        scalar=r[:, h : h + 1],
+                        in1=pairs(table[:, t, w, e, :]),
+                        op0=MULT,
+                        op1=MULT,
+                    )
+            nc.gpsimd.tensor_tensor(out=result, in0=from_even[:], in1=from_odd[:], op=ADD)
+
+        def compute(group):
+            s, b, first_tile, tiles, first_position = group
+            for bank in range(N // BANK):
+                first_head = HEADS_PER_BANK * (bank % BANKS_PER_OUTPUT)
+                rotated = work.tile([P, HEADS_PER_BANK, tiles, HEAD], F32, tag="rotated")
+                for i in range(tiles):
+                    project_norm_rotate(s, first_tile + i, bank, rotated[:, :, i, :])
+                positions = slice(first_position, first_position + tiles * P)
+                nc.sync.dma_start(
+                    out=outputs[bank // BANKS_PER_OUTPUT][
+                        b, first_head : first_head + HEADS_PER_BANK, positions, :
+                    ].rearrange("h (p i) d -> p h (i d)", i=tiles),
+                    in_=rotated[:].rearrange("p h i d -> p h (i d)"),
+                )
+
+        prepare(groups[0])
+        for n, group in enumerate(groups):
+            if n + 1 < len(groups):
+                prepare(groups[n + 1])
+            compute(group)

@@ -12,7 +12,7 @@ FP8X4 = mybir.dt.float8_e4m3fn_x4
 MULT = mybir.AluOpType.mult
 ADD = mybir.AluOpType.add
 SQUARE = mybir.ActivationFunctionType.Square
-SQRT = mybir.ActivationFunctionType.Sqrt
+INVERSE_ROOT = mybir.ActivationFunctionType.Abs_reciprocal_sqrt
 
 P = 128
 BATCH = 2
@@ -63,13 +63,17 @@ def tile_dualstreamattentionwithrotaryembedding_pa_kernel(
     gain_vectors = (qn_x, kn_x, qn_c, kn_c)
     first_gain = {"x": 0, "c": 2}
 
-    groups = [("x", b, X_TILES * b, X_TILES, LEN_C) for b in range(BATCH)]
-    groups += [("c", b, X_TILES * BATCH + b, 1, 0) for b in range(BATCH)]
+    first_position = {"x": LEN_C, "c": 0}
+
+    groups = [("x", [b], X_TILES * b, X_TILES) for b in range(BATCH)]
+    groups += [("c", list(range(BATCH)), X_TILES * BATCH, 1)]
+    vector_sums = {"x": 0, "c": 1}
 
     with ExitStack() as ctx:
         keep = ctx.enter_context(tc.tile_pool(name="keep", bufs=1))
         work = ctx.enter_context(tc.tile_pool(name="work", bufs=3))
         psum = ctx.enter_context(tc.psum_pool(name="psum", bufs=8))
+        ctx.enter_context(tc.manual_schedule())
 
         tokens = keep.tile([P, TOKEN_TILES, K], BF16)
         freqs = keep.tile([P, TOKEN_TILES, HEAD], BF16)
@@ -79,17 +83,20 @@ def tile_dualstreamattentionwithrotaryembedding_pa_kernel(
         ones = keep.tile([P, P], BF16)
         identity = keep.tile([P, P], F32)
 
-        for s in "xc":
-            nc.vector.memset(planes[s][:].bitcast(I32), 0)
         nc.vector.memset(gain_rows[:], 0.0)
         nc.vector.memset(ones[:], 1.0)
+        for s in "xc":
+            nc.vector.memset(planes[s][:].bitcast(I32), 0)
         make_identity(nc, identity[:])
+        warm = keep.tile([P, 1], F32)
+        nc.scalar.activation(out=warm[:], in_=ones[:, 0:1], func=INVERSE_ROOT)
 
         def load_x(b):
-            nc.sync.dma_start(
-                out=tokens[:, X_TILES * b : X_TILES * (b + 1), :],
-                in_=x[b].rearrange("(p i) k -> p i k", i=X_TILES),
-            )
+            for i in range(X_TILES):
+                nc.sync.dma_start(
+                    out=tokens[:, X_TILES * b + i, :],
+                    in_=x[b].rearrange("(p i) k -> p i k", i=X_TILES)[:, i, :],
+                )
 
         def load_scales(s):
             for q in range(4):
@@ -105,29 +112,30 @@ def tile_dualstreamattentionwithrotaryembedding_pa_kernel(
                 in_=given_words[s].rearrange("g p n t -> p g (n t)")[:, :, byte_cols].bitcast(I32),
             )
 
+        for v, vector in enumerate(gain_vectors):
+            nc.sync.dma_start(
+                out=gain_rows[0:1, HEAD * v : HEAD * (v + 1)],
+                in_=vector.rearrange("(o d) -> o d", o=1),
+            )
+        nc.sync.dma_start(
+            out=freqs[:, : X_TILES * BATCH, :].rearrange("p (b i) d -> p b (i d)", b=BATCH),
+            in_=freqs_cis[:, LEN_C:, :, :].rearrange("b (p i) j e -> p b (i j e)", i=X_TILES),
+        )
         load_x(0)
+        load_words("x", 0)
         load_scales("x")
-        for bank in range(N // BANK):
-            load_words("x", bank)
+        nc.sync.dma_start(
+            out=freqs[:, X_TILES * BATCH :, :],
+            in_=freqs_cis[:, :LEN_C, :, :].rearrange("b p j e -> p b (j e)"),
+        )
+        load_words("x", 1)
         load_x(1)
+        load_words("x", 2)
+        load_words("x", 3)
         nc.sync.dma_start(out=tokens[:, X_TILES * BATCH :, :], in_=c.rearrange("b p k -> p b k"))
         load_scales("c")
         for bank in range(N // BANK):
             load_words("c", bank)
-
-        for v, vector in enumerate(gain_vectors):
-            nc.scalar.dma_start(
-                out=gain_rows[0:1, HEAD * v : HEAD * (v + 1)],
-                in_=vector.rearrange("(o d) -> o d", o=1),
-            )
-        nc.scalar.dma_start(
-            out=freqs[:, : X_TILES * BATCH, :].rearrange("p (b i) d -> p b (i d)", b=BATCH),
-            in_=freqs_cis[:, LEN_C:, :, :].rearrange("b (p i) j e -> p b (i j e)", i=X_TILES),
-        )
-        nc.scalar.dma_start(
-            out=freqs[:, X_TILES * BATCH :, :],
-            in_=freqs_cis[:, :LEN_C, :, :].rearrange("b p j e -> p b (j e)"),
-        )
 
         gain_bank = psum.tile([P, BANK], F32, tag="bank")
         nc.tensor.matmul(out=gain_bank[:], lhsT=ones[:], rhs=gain_rows[:], start=True, stop=True)
@@ -135,16 +143,32 @@ def tile_dualstreamattentionwithrotaryembedding_pa_kernel(
         nc.scalar.copy(out=gains[:].rearrange("p v d -> p (v d)"), in_=gain_bank[:])
 
         turned = keep.tile([P, TOKEN_TILES, HEAD], BF16)
-        nc.scalar.mul(out=pairs(turned[:])[:, :, :, 0:1], in_=pairs(freqs[:])[:, :, :, 1:2], mul=-1.0)
-        nc.scalar.copy(out=pairs(turned[:])[:, :, :, 1:2], in_=pairs(freqs[:])[:, :, :, 0:1])
-
         table = keep.tile([P, TOKEN_TILES, 2, 2, HEAD], F32)
         codes = keep.tile([P, TOKEN_TILES, PASSES * P], U32, align_bytes=64)
         code_scales = keep.tile([P, TOKEN_TILES, PASSES * P], U8, align_bytes=64)
 
-        def prepare(group):
-            s, b, first_tile, tiles, first_position = group
-            for t in range(first_tile, first_tile + tiles):
+        def build_tables(group):
+            s, batch_items, first_tile, run = group
+            tiles = len(batch_items) * run
+            these = slice(first_tile, first_tile + tiles)
+            cos_sin = pairs(freqs[:, these, :])
+            partner = pairs(turned[:, these, :])
+            nc.scalar.mul(out=partner[:, :, :, 0:1], in_=cos_sin[:, :, :, 1:2], mul=-1.0)
+            nc.scalar.copy(out=partner[:, :, :, 1:2], in_=cos_sin[:, :, :, 0:1])
+            builder = nc.vector if s == "x" else nc.gpsimd
+            for w in range(2):
+                gain = pairs(gains[:, first_gain[s] + w, :])
+                for e, angles in enumerate((cos_sin, partner)):
+                    builder.tensor_tensor(
+                        out=pairs(table[:, these, w, e, :]),
+                        in0=angles,
+                        in1=gain[:, :, e : e + 1].unsqueeze(1).to_broadcast([P, tiles, PAIRS, 2]),
+                        op=MULT,
+                    )
+
+        def quantise_tokens(group):
+            s, batch_items, first_tile, run = group
+            for t in range(first_tile, first_tile + len(batch_items) * run):
                 token_words = tokens[:, t, :].bitcast(F32)
                 flipped = psum.tile([P, PASSES * 2, P], F32, tag="bank")
                 for g in range(PASSES):
@@ -162,18 +186,8 @@ def tile_dualstreamattentionwithrotaryembedding_pa_kernel(
                 nc.vector.quantize_mx(
                     out=codes[:, t, :].bitcast(FP8X4), scales=code_scales[:, t, :], in_=grouped[:]
                 )
-            these = slice(first_tile, first_tile + tiles)
-            for w in range(2):
-                gain = pairs(gains[:, first_gain[s] + w, :])
-                for e, angles in enumerate((freqs, turned)):
-                    nc.gpsimd.tensor_tensor(
-                        out=pairs(table[:, these, w, e, :]),
-                        in0=pairs(angles[:, these, :]),
-                        in1=gain[:, :, e : e + 1].unsqueeze(1).to_broadcast([P, tiles, PAIRS, 2]),
-                        op=MULT,
-                    )
 
-        def project_norm_rotate(s, t, bank, result):
+        def project_norm_multiply(s, t, bank, from_even, from_odd):
             w = bank // BANKS_PER_OUTPUT
             acc = psum.tile([P, BANK], F32, tag="bank")
             for g in range(PASSES):
@@ -195,12 +209,10 @@ def tile_dualstreamattentionwithrotaryembedding_pa_kernel(
                     func=SQUARE,
                     accum_out=sum_squares[:, h : h + 1],
                 )
-            rms = work.tile([P, HEADS_PER_BANK], F32)
-            nc.scalar.activation(out=rms[:], in_=sum_squares[:], func=SQRT, scale=1.0 / HEAD, bias=EPS)
             r = work.tile([P, HEADS_PER_BANK], F32)
-            nc.vector.reciprocal(out=r[:], in_=rms[:])
-            from_even = work.tile([P, HEADS_PER_BANK, HEAD], F32)
-            from_odd = work.tile([P, HEADS_PER_BANK, HEAD], F32)
+            nc.scalar.activation(
+                out=r[:], in_=sum_squares[:], func=INVERSE_ROOT, scale=1.0 / HEAD, bias=EPS
+            )
             for h in range(HEADS_PER_BANK):
                 head = pairs(acc[:, HEAD * h : HEAD * (h + 1)])
                 for e, product in enumerate((from_even, from_odd)):
@@ -212,25 +224,46 @@ def tile_dualstreamattentionwithrotaryembedding_pa_kernel(
                         op0=MULT,
                         op1=MULT,
                     )
-            nc.gpsimd.tensor_tensor(out=result, in0=from_even[:], in1=from_odd[:], op=ADD)
 
-        def compute(group):
-            s, b, first_tile, tiles, first_position = group
+        def compute(group, next_group):
+            s, batch_items, first_tile, run = group
+            tiles = len(batch_items) * run
+            positions = slice(first_position[s], first_position[s] + run * P)
             for bank in range(N // BANK):
-                first_head = HEADS_PER_BANK * (bank % BANKS_PER_OUTPUT)
-                rotated = work.tile([P, HEADS_PER_BANK, tiles, HEAD], F32, tag="rotated")
-                for i in range(tiles):
-                    project_norm_rotate(s, first_tile + i, bank, rotated[:, :, i, :])
-                positions = slice(first_position, first_position + tiles * P)
-                nc.sync.dma_start(
-                    out=outputs[bank // BANKS_PER_OUTPUT][
-                        b, first_head : first_head + HEADS_PER_BANK, positions, :
-                    ].rearrange("h (p i) d -> p h (i d)", i=tiles),
-                    in_=rotated[:].rearrange("p h i d -> p h (i d)"),
+                heads = slice(
+                    HEADS_PER_BANK * (bank % BANKS_PER_OUTPUT),
+                    HEADS_PER_BANK * (bank % BANKS_PER_OUTPUT + 1),
                 )
+                shape = [P, HEADS_PER_BANK, tiles, HEAD]
+                from_even = work.tile(shape, F32, tag="from_even")
+                from_odd = work.tile(shape, F32, tag="from_odd")
+                rotated = work.tile(shape, F32, tag="rotated")
+                for n in range(tiles):
+                    project_norm_multiply(
+                        s, first_tile + n, bank, from_even[:, :, n, :], from_odd[:, :, n, :]
+                    )
+                split = tiles - vector_sums[s]
+                for engine, first, end in ((nc.gpsimd, 0, split), (nc.vector, split, tiles)):
+                    if first < end:
+                        engine.tensor_tensor(
+                            out=rotated[:, :, first:end, :],
+                            in0=from_even[:, :, first:end, :],
+                            in1=from_odd[:, :, first:end, :],
+                            op=ADD,
+                        )
+                for m, b in enumerate(batch_items):
+                    nc.sync.dma_start(
+                        out=outputs[bank // BANKS_PER_OUTPUT][b, heads, positions, :].rearrange(
+                            "h (p i) d -> p h (i d)", i=run
+                        ),
+                        in_=rotated[:, :, run * m : run * (m + 1), :].rearrange("p h i d -> p h (i d)"),
+                    )
+                if bank == N // BANK // 2 - 1 and next_group is not None:
+                    quantise_tokens(next_group)
 
-        prepare(groups[0])
-        for n, group in enumerate(groups):
-            if n + 1 < len(groups):
-                prepare(groups[n + 1])
-            compute(group)
+        build_tables(groups[0])
+        quantise_tokens(groups[0])
+        for group in groups[1:]:
+            build_tables(group)
+        for group, next_group in zip(groups, groups[1:] + [None]):
+            compute(group, next_group)

@@ -65,9 +65,8 @@ def tile_dualstreamattentionwithrotaryembedding_pa_kernel(
 
     first_position = {"x": LEN_C, "c": 0}
 
-    groups = [("x", [b], X_TILES * b, X_TILES) for b in range(BATCH)]
-    groups += [("c", list(range(BATCH)), X_TILES * BATCH, 1)]
-    vector_sums = {"x": 0, "c": 1}
+    groups = [("x", b, X_TILES * b, X_TILES) for b in range(BATCH)]
+    groups += [("c", b, X_TILES * BATCH + b, 1) for b in range(BATCH)]
 
     with ExitStack() as ctx:
         keep = ctx.enter_context(tc.tile_pool(name="keep", bufs=1))
@@ -121,13 +120,13 @@ def tile_dualstreamattentionwithrotaryembedding_pa_kernel(
             out=freqs[:, : X_TILES * BATCH, :].rearrange("p (b i) d -> p b (i d)", b=BATCH),
             in_=freqs_cis[:, LEN_C:, :, :].rearrange("b (p i) j e -> p b (i j e)", i=X_TILES),
         )
-        load_x(0)
-        load_words("x", 0)
-        load_scales("x")
         nc.sync.dma_start(
             out=freqs[:, X_TILES * BATCH :, :],
             in_=freqs_cis[:, :LEN_C, :, :].rearrange("b p j e -> p b (j e)"),
         )
+        load_x(0)
+        load_words("x", 0)
+        load_scales("x")
         load_words("x", 1)
         load_x(1)
         load_words("x", 2)
@@ -148,18 +147,16 @@ def tile_dualstreamattentionwithrotaryembedding_pa_kernel(
         code_scales = keep.tile([P, TOKEN_TILES, PASSES * P], U8, align_bytes=64)
 
         def build_tables(group):
-            s, batch_items, first_tile, run = group
-            tiles = len(batch_items) * run
+            s, b, first_tile, tiles = group
             these = slice(first_tile, first_tile + tiles)
             cos_sin = pairs(freqs[:, these, :])
             partner = pairs(turned[:, these, :])
             nc.scalar.mul(out=partner[:, :, :, 0:1], in_=cos_sin[:, :, :, 1:2], mul=-1.0)
             nc.scalar.copy(out=partner[:, :, :, 1:2], in_=cos_sin[:, :, :, 0:1])
-            builder = nc.vector if s == "x" else nc.gpsimd
             for w in range(2):
                 gain = pairs(gains[:, first_gain[s] + w, :])
                 for e, angles in enumerate((cos_sin, partner)):
-                    builder.tensor_tensor(
+                    nc.vector.tensor_tensor(
                         out=pairs(table[:, these, w, e, :]),
                         in0=angles,
                         in1=gain[:, :, e : e + 1].unsqueeze(1).to_broadcast([P, tiles, PAIRS, 2]),
@@ -167,8 +164,8 @@ def tile_dualstreamattentionwithrotaryembedding_pa_kernel(
                     )
 
         def quantise_tokens(group):
-            s, batch_items, first_tile, run = group
-            for t in range(first_tile, first_tile + len(batch_items) * run):
+            s, b, first_tile, tiles = group
+            for t in range(first_tile, first_tile + tiles):
                 token_words = tokens[:, t, :].bitcast(F32)
                 flipped = psum.tile([P, PASSES * 2, P], F32, tag="bank")
                 for g in range(PASSES):
@@ -226,9 +223,8 @@ def tile_dualstreamattentionwithrotaryembedding_pa_kernel(
                     )
 
         def compute(group, next_group):
-            s, batch_items, first_tile, run = group
-            tiles = len(batch_items) * run
-            positions = slice(first_position[s], first_position[s] + run * P)
+            s, b, first_tile, tiles = group
+            positions = slice(first_position[s], first_position[s] + tiles * P)
             for bank in range(N // BANK):
                 heads = slice(
                     HEADS_PER_BANK * (bank % BANKS_PER_OUTPUT),
@@ -242,22 +238,13 @@ def tile_dualstreamattentionwithrotaryembedding_pa_kernel(
                     project_norm_multiply(
                         s, first_tile + n, bank, from_even[:, :, n, :], from_odd[:, :, n, :]
                     )
-                split = tiles - vector_sums[s]
-                for engine, first, end in ((nc.gpsimd, 0, split), (nc.vector, split, tiles)):
-                    if first < end:
-                        engine.tensor_tensor(
-                            out=rotated[:, :, first:end, :],
-                            in0=from_even[:, :, first:end, :],
-                            in1=from_odd[:, :, first:end, :],
-                            op=ADD,
-                        )
-                for m, b in enumerate(batch_items):
-                    nc.sync.dma_start(
-                        out=outputs[bank // BANKS_PER_OUTPUT][b, heads, positions, :].rearrange(
-                            "h (p i) d -> p h (i d)", i=run
-                        ),
-                        in_=rotated[:, :, run * m : run * (m + 1), :].rearrange("p h i d -> p h (i d)"),
-                    )
+                nc.gpsimd.tensor_tensor(out=rotated[:], in0=from_even[:], in1=from_odd[:], op=ADD)
+                nc.sync.dma_start(
+                    out=outputs[bank // BANKS_PER_OUTPUT][b, heads, positions, :].rearrange(
+                        "h (p i) d -> p h (i d)", i=tiles
+                    ),
+                    in_=rotated[:].rearrange("p h i d -> p h (i d)"),
+                )
                 if bank == N // BANK // 2 - 1 and next_group is not None:
                     quantise_tokens(next_group)
 

@@ -25,19 +25,15 @@ N = 2048
 HEAD = 128
 PAIRS = HEAD // 2
 BANK = 512
+BANKS = N // BANK
 HEADS_PER_BANK = BANK // HEAD
-BANKS_PER_OUTPUT = N // 2 // BANK
+BANKS_PER_OUTPUT = BANKS // 2
 X_TILES = LEN_X // P
-TOKEN_TILES = BATCH * (X_TILES + 1)
+FIRST_C_TILE = BATCH * X_TILES
+TOKEN_TILES = FIRST_C_TILE + BATCH
 EPS = 1e-6
 
 FLOPS = 2 * BATCH * (LEN_C + LEN_X) * K * N
-
-
-def pairs(ap):
-    if ap.ndim == 2:
-        return ap.rearrange("p (j e) -> p j e", e=2)
-    return ap.rearrange("p t (j e) -> p t j e", e=2)
 
 
 def tile_dualstreamattentionwithrotaryembedding_pa_kernel(
@@ -62,11 +58,10 @@ def tile_dualstreamattentionwithrotaryembedding_pa_kernel(
     given_scales = {"x": Wqk_x_scales, "c": Wqk_c_scales}
     gain_vectors = (qn_x, kn_x, qn_c, kn_c)
     first_gain = {"x": 0, "c": 2}
-
     first_position = {"x": LEN_C, "c": 0}
 
     groups = [("x", b, X_TILES * b, X_TILES) for b in range(BATCH)]
-    groups += [("c", b, X_TILES * BATCH + b, 1) for b in range(BATCH)]
+    groups += [("c", b, FIRST_C_TILE + b, 1) for b in range(BATCH)]
 
     with ExitStack() as ctx:
         keep = ctx.enter_context(tc.tile_pool(name="keep", bufs=1))
@@ -75,7 +70,7 @@ def tile_dualstreamattentionwithrotaryembedding_pa_kernel(
         ctx.enter_context(tc.manual_schedule())
 
         tokens = keep.tile([P, TOKEN_TILES, K], BF16)
-        freqs = keep.tile([P, TOKEN_TILES, HEAD], BF16)
+        angles = keep.tile([P, TOKEN_TILES, 2, HEAD], BF16)
         words = {s: keep.tile([P, PASSES, 4 * N], U8, name="words_" + s, align_bytes=64) for s in "xc"}
         planes = {s: keep.tile([P, N], U8, name="planes_" + s, align_bytes=64) for s in "xc"}
         gain_rows = keep.tile([P, len(gain_vectors) * HEAD], BF16)
@@ -97,6 +92,12 @@ def tile_dualstreamattentionwithrotaryembedding_pa_kernel(
                     in_=x[b].rearrange("(p i) k -> p i k", i=X_TILES)[:, i, :],
                 )
 
+        def load_x_angles(b):
+            nc.sync.dma_start(
+                out=angles[:, X_TILES * b : X_TILES * (b + 1), 0, :],
+                in_=freqs_cis[b, LEN_C:, :, :].rearrange("(p i) j e -> p i (j e)", i=X_TILES),
+            )
+
         def load_scales(s):
             for q in range(4):
                 nc.sync.dma_start(
@@ -111,29 +112,27 @@ def tile_dualstreamattentionwithrotaryembedding_pa_kernel(
                 in_=given_words[s].rearrange("g p n t -> p g (n t)")[:, :, byte_cols].bitcast(I32),
             )
 
+        load_x_angles(0)
         for v, vector in enumerate(gain_vectors):
             nc.sync.dma_start(
                 out=gain_rows[0:1, HEAD * v : HEAD * (v + 1)],
                 in_=vector.rearrange("(o d) -> o d", o=1),
             )
-        nc.sync.dma_start(
-            out=freqs[:, : X_TILES * BATCH, :].rearrange("p (b i) d -> p b (i d)", b=BATCH),
-            in_=freqs_cis[:, LEN_C:, :, :].rearrange("b (p i) j e -> p b (i j e)", i=X_TILES),
-        )
-        nc.sync.dma_start(
-            out=freqs[:, X_TILES * BATCH :, :],
-            in_=freqs_cis[:, :LEN_C, :, :].rearrange("b p j e -> p b (j e)"),
-        )
         load_x(0)
         load_words("x", 0)
         load_scales("x")
+        load_x_angles(1)
+        nc.sync.dma_start(
+            out=angles[:, FIRST_C_TILE:, 0, :],
+            in_=freqs_cis[:, :LEN_C, :, :].rearrange("b p j e -> p b (j e)"),
+        )
         load_words("x", 1)
         load_x(1)
         load_words("x", 2)
         load_words("x", 3)
-        nc.sync.dma_start(out=tokens[:, X_TILES * BATCH :, :], in_=c.rearrange("b p k -> p b k"))
+        nc.sync.dma_start(out=tokens[:, FIRST_C_TILE:, :], in_=c.rearrange("b p k -> p b k"))
         load_scales("c")
-        for bank in range(N // BANK):
+        for bank in range(BANKS):
             load_words("c", bank)
 
         gain_bank = psum.tile([P, BANK], F32, tag="bank")
@@ -141,30 +140,30 @@ def tile_dualstreamattentionwithrotaryembedding_pa_kernel(
         gains = keep.tile([P, len(gain_vectors), HEAD], F32)
         nc.scalar.copy(out=gains[:].rearrange("p v d -> p (v d)"), in_=gain_bank[:])
 
-        turned = keep.tile([P, TOKEN_TILES, HEAD], BF16)
-        table = keep.tile([P, TOKEN_TILES, 2, 2, HEAD], F32)
+        table = keep.tile([P, TOKEN_TILES, 2, 2 * HEAD], F32)
         codes = keep.tile([P, TOKEN_TILES, PASSES * P], U32, align_bytes=64)
         code_scales = keep.tile([P, TOKEN_TILES, PASSES * P], U8, align_bytes=64)
 
         def build_tables(group):
-            s, b, first_tile, tiles = group
+            stream, b, first_tile, tiles = group
             these = slice(first_tile, first_tile + tiles)
-            cos_sin = pairs(freqs[:, these, :])
-            partner = pairs(turned[:, these, :])
-            nc.scalar.mul(out=partner[:, :, :, 0:1], in_=cos_sin[:, :, :, 1:2], mul=-1.0)
-            nc.scalar.copy(out=partner[:, :, :, 1:2], in_=cos_sin[:, :, :, 0:1])
-            for w in range(2):
-                gain = pairs(gains[:, first_gain[s] + w, :])
-                for e, angles in enumerate((cos_sin, partner)):
-                    nc.vector.tensor_tensor(
-                        out=pairs(table[:, these, w, e, :]),
-                        in0=angles,
-                        in1=gain[:, :, e : e + 1].unsqueeze(1).to_broadcast([P, tiles, PAIRS, 2]),
+            given = angles[:, these, 0, :].rearrange("p t (j e) -> p t j e", e=2)
+            turned = angles[:, these, 1, :].rearrange("p t (j e) -> p t j e", e=2)
+            nc.scalar.mul(out=turned[:, :, :, 0:1], in_=given[:, :, :, 1:2], mul=-1.0)
+            nc.scalar.copy(out=turned[:, :, :, 1:2], in_=given[:, :, :, 0:1])
+            builder = nc.vector if stream == "x" else nc.gpsimd
+            for t in range(first_tile, first_tile + tiles):
+                for w in range(2):
+                    gain = gains[:, first_gain[stream] + w, :].rearrange("p (j o) -> p j o", o=2)
+                    builder.tensor_tensor(
+                        out=table[:, t, w, :].rearrange("p (j o e) -> p j o e", o=2, e=2),
+                        in0=angles[:, t, :, :].rearrange("p o (j e) -> p j o e", e=2),
+                        in1=gain.unsqueeze(3).to_broadcast([P, PAIRS, 2, 2]),
                         op=MULT,
                     )
 
         def quantise_tokens(group):
-            s, b, first_tile, tiles = group
+            stream, b, first_tile, tiles = group
             for t in range(first_tile, first_tile + tiles):
                 token_words = tokens[:, t, :].bitcast(F32)
                 flipped = psum.tile([P, PASSES * 2, P], F32, tag="bank")
@@ -184,16 +183,15 @@ def tile_dualstreamattentionwithrotaryembedding_pa_kernel(
                     out=codes[:, t, :].bitcast(FP8X4), scales=code_scales[:, t, :], in_=grouped[:]
                 )
 
-        def project_norm_multiply(s, t, bank, from_even, from_odd):
-            w = bank // BANKS_PER_OUTPUT
+        def project_norm_multiply(stream, t, bank, products):
             acc = psum.tile([P, BANK], F32, tag="bank")
             for g in range(PASSES):
                 nc.tensor.matmul_mx(
                     out=acc[:],
                     lhsT=codes[:, t, P * g : P * (g + 1)].bitcast(FP8X4),
                     lhsT_scale=code_scales[:, t, P * g : P * (g + 1)],
-                    rhs=words[s][:, g, 4 * BANK * bank : 4 * BANK * (bank + 1)].bitcast(FP8X4),
-                    rhs_scale=planes[s][4 * g : P, BANK * bank : BANK * (bank + 1)],
+                    rhs=words[stream][:, g, 4 * BANK * bank : 4 * BANK * (bank + 1)].bitcast(FP8X4),
+                    rhs_scale=planes[stream][4 * g : P, BANK * bank : BANK * (bank + 1)],
                     start=(g == 0),
                     stop=(g == PASSES - 1),
                 )
@@ -211,41 +209,41 @@ def tile_dualstreamattentionwithrotaryembedding_pa_kernel(
                 out=r[:], in_=sum_squares[:], func=INVERSE_ROOT, scale=1.0 / HEAD, bias=EPS
             )
             for h in range(HEADS_PER_BANK):
-                head = pairs(acc[:, HEAD * h : HEAD * (h + 1)])
-                for e, product in enumerate((from_even, from_odd)):
-                    nc.vector.scalar_tensor_tensor(
-                        out=pairs(product[:, h, :]),
-                        in0=head[:, :, e : e + 1].to_broadcast([P, PAIRS, 2]),
-                        scalar=r[:, h : h + 1],
-                        in1=pairs(table[:, t, w, e, :]),
-                        op0=MULT,
-                        op1=MULT,
-                    )
+                nc.vector.scalar_tensor_tensor(
+                    out=products[:, h, :].rearrange("p (d e) -> p d e", e=2),
+                    in0=acc[:, HEAD * h : HEAD * (h + 1)].unsqueeze(2).to_broadcast([P, HEAD, 2]),
+                    scalar=r[:, h : h + 1],
+                    in1=table[:, t, bank // BANKS_PER_OUTPUT, :].rearrange("p (d e) -> p d e", e=2),
+                    op0=MULT,
+                    op1=MULT,
+                )
 
         def compute(group, next_group):
-            s, b, first_tile, tiles = group
-            positions = slice(first_position[s], first_position[s] + tiles * P)
-            for bank in range(N // BANK):
+            stream, b, first_tile, tiles = group
+            positions = slice(first_position[stream], first_position[stream] + tiles * P)
+            for bank in range(BANKS):
                 heads = slice(
                     HEADS_PER_BANK * (bank % BANKS_PER_OUTPUT),
                     HEADS_PER_BANK * (bank % BANKS_PER_OUTPUT + 1),
                 )
-                shape = [P, HEADS_PER_BANK, tiles, HEAD]
-                from_even = work.tile(shape, F32, tag="from_even")
-                from_odd = work.tile(shape, F32, tag="from_odd")
-                rotated = work.tile(shape, F32, tag="rotated")
-                for n in range(tiles):
-                    project_norm_multiply(
-                        s, first_tile + n, bank, from_even[:, :, n, :], from_odd[:, :, n, :]
-                    )
-                nc.gpsimd.tensor_tensor(out=rotated[:], in0=from_even[:], in1=from_odd[:], op=ADD)
+                products = work.tile([P, HEADS_PER_BANK, tiles, 2 * HEAD], F32, tag="products")
+                rotated = work.tile([P, HEADS_PER_BANK, tiles, HEAD], F32, tag="rotated")
+                for i in range(tiles):
+                    project_norm_multiply(stream, first_tile + i, bank, products[:, :, i, :])
+                by_source = products[:].rearrange("p h i (j o e) -> p (h i j) o e", o=2, e=2)
+                nc.gpsimd.tensor_tensor(
+                    out=rotated[:].rearrange("p h i (j e) -> p (h i j) e", e=2),
+                    in0=by_source[:, :, 0, :],
+                    in1=by_source[:, :, 1, :],
+                    op=ADD,
+                )
                 nc.sync.dma_start(
                     out=outputs[bank // BANKS_PER_OUTPUT][b, heads, positions, :].rearrange(
                         "h (p i) d -> p h (i d)", i=tiles
                     ),
                     in_=rotated[:].rearrange("p h i d -> p h (i d)"),
                 )
-                if bank == N // BANK // 2 - 1 and next_group is not None:
+                if bank == BANKS // 2 - 1 and next_group is not None:
                     quantise_tokens(next_group)
 
         build_tables(groups[0])

@@ -162,8 +162,7 @@ def tile_dualstreamattentionwithrotaryembedding_pa_kernel(
                         op=MULT,
                     )
 
-        def quantise_tokens(group):
-            stream, b, first_tile, tiles = group
+        def quantise_tokens(first_tile, tiles):
             for t in range(first_tile, first_tile + tiles):
                 token_words = tokens[:, t, :].bitcast(F32)
                 flipped = psum.tile([P, PASSES * 2, P], F32, tag="bank")
@@ -243,11 +242,11 @@ def tile_dualstreamattentionwithrotaryembedding_pa_kernel(
                     ),
                     in_=rotated[:].rearrange("p h i d -> p h (i d)"),
                 )
-                if bank == BANKS // 2 - 1 and next_group is not None:
-                    quantise_tokens(next_group)
+                if next_group is not None and bank < next_group[3]:
+                    quantise_tokens(next_group[2] + bank, 1)
 
         build_tables(groups[0])
-        quantise_tokens(groups[0])
+        quantise_tokens(groups[0][2], groups[0][3])
         for group in groups[1:]:
             build_tables(group)
         for group, next_group in zip(groups, groups[1:] + [None]):

@@ -137,8 +137,9 @@ def tile_dualstreamattentionwithrotaryembedding_pa_kernel(
 
         gain_bank = psum.tile([P, BANK], F32, tag="bank")
         nc.tensor.matmul(out=gain_bank[:], lhsT=ones[:], rhs=gain_rows[:], start=True, stop=True)
-        gains = keep.tile([P, len(gain_vectors), HEAD], F32)
-        nc.scalar.copy(out=gains[:].rearrange("p v d -> p (v d)"), in_=gain_bank[:])
+        gains_c = keep.tile([P, 2 * HEAD], F32)
+        nc.scalar.copy(out=gains_c[:], in_=gain_bank[:, HEAD * first_gain["c"] :])
+        gains = {"x": gain_bank[:, : 2 * HEAD], "c": gains_c[:]}
 
         table = keep.tile([P, TOKEN_TILES, 2, 2 * HEAD], F32)
         codes = keep.tile([P, TOKEN_TILES, PASSES * P], U32, align_bytes=64)
@@ -154,7 +155,7 @@ def tile_dualstreamattentionwithrotaryembedding_pa_kernel(
             builder = nc.vector if stream == "x" else nc.gpsimd
             for t in range(first_tile, first_tile + tiles):
                 for w in range(2):
-                    gain = gains[:, first_gain[stream] + w, :].rearrange("p (j o) -> p j o", o=2)
+                    gain = gains[stream][:, HEAD * w : HEAD * (w + 1)].rearrange("p (j o) -> p j o", o=2)
                     builder.tensor_tensor(
                         out=table[:, t, w, :].rearrange("p (j o e) -> p j o e", o=2, e=2),
                         in0=angles[:, t, :, :].rearrange("p o (j e) -> p j o e", e=2),

@@ -66,6 +66,7 @@ def tile_dualstreamattentionwithrotaryembedding_pa_kernel(
     with ExitStack() as ctx:
         keep = ctx.enter_context(tc.tile_pool(name="keep", bufs=1))
         work = ctx.enter_context(tc.tile_pool(name="work", bufs=3))
+        leaving = ctx.enter_context(tc.tile_pool(name="leaving", bufs=6))
         psum = ctx.enter_context(tc.psum_pool(name="psum", bufs=8))
         ctx.enter_context(tc.manual_schedule())
 
@@ -227,7 +228,7 @@ def tile_dualstreamattentionwithrotaryembedding_pa_kernel(
                     HEADS_PER_BANK * (bank % BANKS_PER_OUTPUT + 1),
                 )
                 products = work.tile([P, HEADS_PER_BANK, tiles, 2 * HEAD], F32, tag="products")
-                rotated = work.tile([P, HEADS_PER_BANK, tiles, HEAD], F32, tag="rotated")
+                rotated = leaving.tile([P, HEADS_PER_BANK, tiles, HEAD], F32, tag="rotated")
                 for i in range(tiles):
                     project_norm_multiply(stream, first_tile + i, bank, products[:, :, i, :])
                 by_source = products[:].rearrange("p h i (j o e) -> p (h i j) o e", o=2, e=2)

@@ -33,6 +33,8 @@ FIRST_C_TILE = BATCH * X_TILES
 TOKEN_TILES = FIRST_C_TILE + BATCH
 EPS = 1e-6
 
+LEFT_TO_VECTOR = 2
+
 FLOPS = 2 * BATCH * (LEN_C + LEN_X) * K * N
 
 
@@ -65,7 +67,7 @@ def tile_dualstreamattentionwithrotaryembedding_pa_kernel(
 
     with ExitStack() as ctx:
         keep = ctx.enter_context(tc.tile_pool(name="keep", bufs=1))
-        work = ctx.enter_context(tc.tile_pool(name="work", bufs=3))
+        work = ctx.enter_context(tc.tile_pool(name="work", bufs=5))
         leaving = ctx.enter_context(tc.tile_pool(name="leaving", bufs=6))
         psum = ctx.enter_context(tc.psum_pool(name="psum", bufs=8))
         ctx.enter_context(tc.manual_schedule())
@@ -219,6 +221,23 @@ def tile_dualstreamattentionwithrotaryembedding_pa_kernel(
                     op1=MULT,
                 )
 
+        def add_and_store(engine, products, rotated, b, bank, heads, positions, tiles):
+            by_source = products[:].rearrange("p h i (j o e) -> p (h i j) o e", o=2, e=2)
+            engine.tensor_tensor(
+                out=rotated[:].rearrange("p h i (j e) -> p (h i j) e", e=2),
+                in0=by_source[:, :, 0, :],
+                in1=by_source[:, :, 1, :],
+                op=ADD,
+            )
+            nc.sync.dma_start(
+                out=outputs[bank // BANKS_PER_OUTPUT][b, heads, positions, :].rearrange(
+                    "h (p i) d -> p h (i d)", i=tiles
+                ),
+                in_=rotated[:].rearrange("p h i d -> p h (i d)"),
+            )
+
+        left_to_vector = []
+
         def compute(group, next_group):
             stream, b, first_tile, tiles = group
             positions = slice(first_position[stream], first_position[stream] + tiles * P)
@@ -231,19 +250,11 @@ def tile_dualstreamattentionwithrotaryembedding_pa_kernel(
                 rotated = leaving.tile([P, HEADS_PER_BANK, tiles, HEAD], F32, tag="rotated")
                 for i in range(tiles):
                     project_norm_multiply(stream, first_tile + i, bank, products[:, :, i, :])
-                by_source = products[:].rearrange("p h i (j o e) -> p (h i j) o e", o=2, e=2)
-                nc.gpsimd.tensor_tensor(
-                    out=rotated[:].rearrange("p h i (j e) -> p (h i j) e", e=2),
-                    in0=by_source[:, :, 0, :],
-                    in1=by_source[:, :, 1, :],
-                    op=ADD,
-                )
-                nc.sync.dma_start(
-                    out=outputs[bank // BANKS_PER_OUTPUT][b, heads, positions, :].rearrange(
-                        "h (p i) d -> p h (i d)", i=tiles
-                    ),
-                    in_=rotated[:].rearrange("p h i d -> p h (i d)"),
-                )
+                leftover = next_group is None and bank >= BANKS - LEFT_TO_VECTOR
+                if leftover:
+                    left_to_vector.append((products, rotated, bank, heads))
+                else:
+                    add_and_store(nc.gpsimd, products, rotated, b, bank, heads, positions, tiles)
                 if next_group is not None and bank < next_group[3]:
                     quantise_tokens(next_group[2] + bank, 1)
 
@@ -253,3 +264,7 @@ def tile_dualstreamattentionwithrotaryembedding_pa_kernel(
             build_tables(group)
         for group, next_group in zip(groups, groups[1:] + [None]):
             compute(group, next_group)
+        stream, b, first_tile, tiles = groups[-1]
+        for products, rotated, bank, heads in left_to_vector:
+            positions = slice(first_position[stream], first_position[stream] + tiles * P)
+            add_and_store(nc.vector, products, rotated, b, bank, heads, positions, tiles)

from contextlib import ExitStack

import concourse.mybir as mybir
from concourse.masks import make_identity

F32 = mybir.dt.float32
BF16 = mybir.dt.bfloat16
I32 = mybir.dt.int32
U32 = mybir.dt.uint32
U8 = mybir.dt.uint8
FP8X4 = mybir.dt.float8_e4m3fn_x4
MULT = mybir.AluOpType.mult
ADD = mybir.AluOpType.add
SQUARE = mybir.ActivationFunctionType.Square
INVERSE_ROOT = mybir.ActivationFunctionType.Abs_reciprocal_sqrt

P = 128
BATCH = 2
LEN_C = 128
LEN_X = 384
K = 1024
K_PASS = 512
PASSES = K // K_PASS
N = 2048
HEAD = 128
PAIRS = HEAD // 2
BANK = 512
BANKS = N // BANK
HEADS_PER_BANK = BANK // HEAD
BANKS_PER_OUTPUT = BANKS // 2
X_TILES = LEN_X // P
FIRST_C_TILE = BATCH * X_TILES
TOKEN_TILES = FIRST_C_TILE + BATCH
EPS = 1e-6

LEFT_TO_VECTOR = 2

FLOPS = 2 * BATCH * (LEN_C + LEN_X) * K * N


def tile_dualstreamattentionwithrotaryembedding_pa_kernel(
    tc,
    x,
    c,
    freqs_cis,
    Wqk_x_words,
    Wqk_x_scales,
    qn_x,
    kn_x,
    Wqk_c_words,
    Wqk_c_scales,
    qn_c,
    kn_c,
    out_0,
    out_1,
):
    nc = tc.nc
    outputs = (out_0, out_1)
    given_words = {"x": Wqk_x_words, "c": Wqk_c_words}
    given_scales = {"x": Wqk_x_scales, "c": Wqk_c_scales}
    gain_vectors = (qn_x, kn_x, qn_c, kn_c)
    first_gain = {"x": 0, "c": 2}
    first_position = {"x": LEN_C, "c": 0}

    groups = [("x", b, X_TILES * b, X_TILES) for b in range(BATCH)]
    groups += [("c", b, FIRST_C_TILE + b, 1) for b in range(BATCH)]

    with ExitStack() as ctx:
        keep = ctx.enter_context(tc.tile_pool(name="keep", bufs=1))
        work = ctx.enter_context(tc.tile_pool(name="work", bufs=5))
        leaving = ctx.enter_context(tc.tile_pool(name="leaving", bufs=6))
        psum = ctx.enter_context(tc.psum_pool(name="psum", bufs=8))
        ctx.enter_context(tc.manual_schedule())

        tokens = keep.tile([P, TOKEN_TILES, K], BF16)
        angles = keep.tile([P, TOKEN_TILES, 2, HEAD], BF16)
        words = {s: keep.tile([P, PASSES, 4 * N], U8, name="words_" + s, align_bytes=64) for s in "xc"}
        planes = {s: keep.tile([P, N], U8, name="planes_" + s, align_bytes=64) for s in "xc"}
        gain_rows = keep.tile([P, len(gain_vectors) * HEAD], BF16)
        ones = keep.tile([P, P], BF16)
        identity = keep.tile([P, P], F32)

        nc.vector.memset(gain_rows[:], 0.0)
        nc.vector.memset(ones[:], 1.0)
        for s in "xc":
            nc.vector.memset(planes[s][:].bitcast(I32), 0)
        make_identity(nc, identity[:])
        warm = keep.tile([P, 1], F32)
        nc.scalar.activation(out=warm[:], in_=ones[:, 0:1], func=INVERSE_ROOT)

        def load_x(b):
            for i in range(X_TILES):
                nc.sync.dma_start(
                    out=tokens[:, X_TILES * b + i, :],
                    in_=x[b].rearrange("(p i) k -> p i k", i=X_TILES)[:, i, :],
                )

        def load_x_angles(b):
            nc.sync.dma_start(
                out=angles[:, X_TILES * b : X_TILES * (b + 1), 0, :],
                in_=freqs_cis[b, LEN_C:, :, :].rearrange("(p i) j e -> p i (j e)", i=X_TILES),
            )

        def load_scales(s):
            for q in range(4):
                nc.sync.dma_start(
                    out=planes[s][32 * q : 32 * q + 4 * PASSES, :].bitcast(I32),
                    in_=given_scales[s][:, 4 * q : 4 * q + 4, :].bitcast(I32),
                )

        def load_words(s, bank):
            byte_cols = slice(4 * BANK * bank, 4 * BANK * (bank + 1))
            nc.sync.dma_start(
                out=words[s][:, :, byte_cols].bitcast(I32),
                in_=given_words[s].rearrange("g p n t -> p g (n t)")[:, :, byte_cols].bitcast(I32),
            )

        load_x_angles(0)
        for v, vector in enumerate(gain_vectors):
            nc.sync.dma_start(
                out=gain_rows[0:1, HEAD * v : HEAD * (v + 1)],
                in_=vector.rearrange("(o d) -> o d", o=1),
            )
        load_x(0)
        load_words("x", 0)
        load_scales("x")
        load_x_angles(1)
        nc.sync.dma_start(
            out=angles[:, FIRST_C_TILE:, 0, :],
            in_=freqs_cis[:, :LEN_C, :, :].rearrange("b p j e -> p b (j e)"),
        )
        load_words("x", 1)
        load_x(1)
        load_words("x", 2)
        load_words("x", 3)
        nc.sync.dma_start(out=tokens[:, FIRST_C_TILE:, :], in_=c.rearrange("b p k -> p b k"))
        load_scales("c")
        for bank in range(BANKS):
            load_words("c", bank)

        gain_bank = psum.tile([P, BANK], F32, tag="bank")
        nc.tensor.matmul(out=gain_bank[:], lhsT=ones[:], rhs=gain_rows[:], start=True, stop=True)
        gains_c = keep.tile([P, 2 * HEAD], F32)
        nc.scalar.copy(out=gains_c[:], in_=gain_bank[:, HEAD * first_gain["c"] :])
        gains = {"x": gain_bank[:, : 2 * HEAD], "c": gains_c[:]}

        table = keep.tile([P, TOKEN_TILES, 2, 2 * HEAD], F32)
        codes = keep.tile([P, TOKEN_TILES, PASSES * P], U32, align_bytes=64)
        code_scales = keep.tile([P, TOKEN_TILES, PASSES * P], U8, align_bytes=64)

        def build_tables(group):
            stream, b, first_tile, tiles = group
            these = slice(first_tile, first_tile + tiles)
            given = angles[:, these, 0, :].rearrange("p t (j e) -> p t j e", e=2)
            turned = angles[:, these, 1, :].rearrange("p t (j e) -> p t j e", e=2)
            nc.scalar.mul(out=turned[:, :, :, 0:1], in_=given[:, :, :, 1:2], mul=-1.0)
            nc.scalar.copy(out=turned[:, :, :, 1:2], in_=given[:, :, :, 0:1])
            builder = nc.vector if stream == "x" else nc.gpsimd
            for t in range(first_tile, first_tile + tiles):
                for w in range(2):
                    gain = gains[stream][:, HEAD * w : HEAD * (w + 1)].rearrange("p (j o) -> p j o", o=2)
                    builder.tensor_tensor(
                        out=table[:, t, w, :].rearrange("p (j o e) -> p j o e", o=2, e=2),
                        in0=angles[:, t, :, :].rearrange("p o (j e) -> p j o e", e=2),
                        in1=gain.unsqueeze(3).to_broadcast([P, PAIRS, 2, 2]),
                        op=MULT,
                    )

        def quantise_tokens(first_tile, tiles):
            for t in range(first_tile, first_tile + tiles):
                token_words = tokens[:, t, :].bitcast(F32)
                flipped = psum.tile([P, PASSES * 2, P], F32, tag="bank")
                for g in range(PASSES):
                    for u in range(2):
                        nc.tensor.transpose(
                            flipped[:, 2 * g + u, :],
                            token_words[:, 256 * g + u : 256 * (g + 1) : 2],
                            identity[:],
                        )
                grouped = work.tile([P, K], BF16, align_bytes=64)
                nc.scalar.copy(
                    out=grouped[:].bitcast(F32).rearrange("p (g r u) -> p g r u", g=PASSES, u=2),
                    in_=flipped[:].rearrange("p (g u) r -> p g r u", u=2),
                )
                nc.vector.quantize_mx(
                    out=codes[:, t, :].bitcast(FP8X4), scales=code_scales[:, t, :], in_=grouped[:]
                )

        def project_norm_multiply(stream, t, bank, products):
            acc = psum.tile([P, BANK], F32, tag="bank")
            for g in range(PASSES):
                nc.tensor.matmul_mx(
                    out=acc[:],
                    lhsT=codes[:, t, P * g : P * (g + 1)].bitcast(FP8X4),
                    lhsT_scale=code_scales[:, t, P * g : P * (g + 1)],
                    rhs=words[stream][:, g, 4 * BANK * bank : 4 * BANK * (bank + 1)].bitcast(FP8X4),
                    rhs_scale=planes[stream][4 * g : P, BANK * bank : BANK * (bank + 1)],
                    start=(g == 0),
                    stop=(g == PASSES - 1),
                )
            squares = work.tile([P, BANK], F32)
            sum_squares = work.tile([P, HEADS_PER_BANK], F32)
            for h in range(HEADS_PER_BANK):
                nc.scalar.activation(
                    out=squares[:, HEAD * h : HEAD * (h + 1)],
                    in_=acc[:, HEAD * h : HEAD * (h + 1)],
                    func=SQUARE,
                    accum_out=sum_squares[:, h : h + 1],
                )
            r = work.tile([P, HEADS_PER_BANK], F32)
            nc.scalar.activation(
                out=r[:], in_=sum_squares[:], func=INVERSE_ROOT, scale=1.0 / HEAD, bias=EPS
            )
            for h in range(HEADS_PER_BANK):
                nc.vector.scalar_tensor_tensor(
                    out=products[:, h, :].rearrange("p (d e) -> p d e", e=2),
                    in0=acc[:, HEAD * h : HEAD * (h + 1)].unsqueeze(2).to_broadcast([P, HEAD, 2]),
                    scalar=r[:, h : h + 1],
                    in1=table[:, t, bank // BANKS_PER_OUTPUT, :].rearrange("p (d e) -> p d e", e=2),
                    op0=MULT,
                    op1=MULT,
                )

        def add_and_store(engine, products, rotated, b, bank, heads, positions, tiles):
            by_source = products[:].rearrange("p h i (j o e) -> p (h i j) o e", o=2, e=2)
            engine.tensor_tensor(
                out=rotated[:].rearrange("p h i (j e) -> p (h i j) e", e=2),
                in0=by_source[:, :, 0, :],
                in1=by_source[:, :, 1, :],
                op=ADD,
            )
            nc.sync.dma_start(
                out=outputs[bank // BANKS_PER_OUTPUT][b, heads, positions, :].rearrange(
                    "h (p i) d -> p h (i d)", i=tiles
                ),
                in_=rotated[:].rearrange("p h i d -> p h (i d)"),
            )

        left_to_vector = []

        def compute(group, next_group):
            stream, b, first_tile, tiles = group
            positions = slice(first_position[stream], first_position[stream] + tiles * P)
            for bank in range(BANKS):
                heads = slice(
                    HEADS_PER_BANK * (bank % BANKS_PER_OUTPUT),
                    HEADS_PER_BANK * (bank % BANKS_PER_OUTPUT + 1),
                )
                products = work.tile([P, HEADS_PER_BANK, tiles, 2 * HEAD], F32, tag="products")
                rotated = leaving.tile([P, HEADS_PER_BANK, tiles, HEAD], F32, tag="rotated")
                for i in range(tiles):
                    project_norm_multiply(stream, first_tile + i, bank, products[:, :, i, :])
                leftover = next_group is None and bank >= BANKS - LEFT_TO_VECTOR
                if leftover:
                    left_to_vector.append((products, rotated, bank, heads))
                else:
                    add_and_store(nc.gpsimd, products, rotated, b, bank, heads, positions, tiles)
                if next_group is not None and bank < next_group[3]:
                    quantise_tokens(next_group[2] + bank, 1)

        build_tables(groups[0])
        quantise_tokens(groups[0][2], groups[0][3])
        for group in groups[1:]:
            build_tables(group)
        for group, next_group in zip(groups, groups[1:] + [None]):
            compute(group, next_group)
        stream, b, first_tile, tiles = groups[-1]
        for products, rotated, bank, heads in left_to_vector:
            positions = slice(first_position[stream], first_position[stream] + tiles * P)
            add_and_store(nc.vector, products, rotated, b, bank, heads, positions, tiles)
